import numpy as np
import ml_dtypes


def mxq(x, axis, fmt="e4m3"):
    dtype, down = {"e4m3": (ml_dtypes.float8_e4m3fn, 7), "e5m2": (ml_dtypes.float8_e5m2, 14)}[fmt]
    v = np.moveaxis(np.asarray(x, np.float32).astype(ml_dtypes.bfloat16).astype(np.float64), axis, -1)
    blocks = v.reshape(v.shape[:-1] + (-1, 32))
    amax = np.abs(blocks).max(-1, keepdims=True)
    byte = np.maximum(np.where(amax > 0, np.frexp(amax)[1] - 1 + 127, 0) - down, 1)
    scale = np.exp2(byte - 127.0)
    codes = (blocks / scale).astype(np.float32).astype(dtype).astype(np.float64)
    return np.moveaxis((codes * scale).reshape(v.shape), -1, axis)


WIDE = False


def mx_kscale(k):
    if not WIDE:
        return np.ones(k)
    levels = np.array([10, -10, 5, -5, 0])
    a = np.random.permutation(np.resize(levels, k // 512 * 4)).reshape(k // 512, 4)
    idx = np.arange(k)
    return np.exp2(a[idx // 512, idx % 128 // 32])


BF16 = ml_dtypes.bfloat16


def bf(x):
    return np.asarray(x, np.float32).astype(BF16)


def f64(x):
    return np.asarray(x).astype(np.float64)


B, N, R, I = 16, 512, 128, 256
SIG = 1.5
P0 = 0.05
RM = np.exp(0.5 * SIG * SIG)


def draw_flows():
    keep = np.random.random((B, 1, N)) >= P0
    return keep * np.exp(SIG * np.random.standard_normal((B, N, N)) - 0.5 * SIG * SIG)


def setup_inputs():
    u = mx_kscale(N)
    return {"flows": bf(draw_flows() * u[None, :, None]),
            "x_gcn1": bf(np.random.standard_normal((B, N, R)) / u[None, :, None] * np.mean(u)),
            "W2": bf(np.random.standard_normal((R, I)) * 0.5 * np.sqrt(N) / (RM * np.sqrt(R))),
            "b2": bf(np.random.standard_normal(I) * 0.1)}


def reference(flows, x_gcn1, W2, b2):
    A = f64(flows)
    deg = A.sum(axis=1)
    dinv = np.where(deg > 0, 1.0 / np.sqrt(np.where(deg > 0, deg, 1.0)), 0.0)
    xw = f64(x_gcn1) @ f64(W2)
    msg = xw * dinv[..., None]
    out = mxq(A, 1, "e4m3").transpose(0, 2, 1) @ mxq(msg, 1, "e4m3")
    return out * dinv[..., None] + f64(b2)

@@ -1,0 +1,337 @@
+from contextlib import ExitStack
+
+import concourse.mybir as mybir
+from concourse.masks import make_identity
+
+F32 = mybir.dt.float32
+BF16 = mybir.dt.bfloat16
+U32 = mybir.dt.uint32
+U8 = mybir.dt.uint8
+FP8X4 = mybir.dt.float8_e4m3fn_x4
+ALU = mybir.AluOpType
+ACT = mybir.ActivationFunctionType
+AXIS = mybir.AxisListType
+
+GRAPHS = 16
+NODES = 512
+FEAT = 128
+WIDTH = 256
+P = 128
+PACK = 4
+QUARTER = P // PACK
+
+FLOPS = 2 * GRAPHS * NODES * FEAT * WIDTH + 2 * GRAPHS * NODES * NODES * WIDTH
+
+GROUP = 4
+
+VECTOR_COLUMNS = 48
+
+QUANTISE_LAG = 1
+LANES_LAG = 1
+ROOT_LAG = 2
+TRANSPOSE_LAG = GROUP
+COPY_LAG = GROUP + 1
+MESSAGE_LAG = GROUP + 2
+PACK_LAG = GROUP + 3
+OUTPUT_LAG = GROUP + 5
+
+
+def tile_encoder_flows_pb_t_kernel(tc, flows, x_gcn1, W2, b2, out):
+    nc = tc.nc
+    with ExitStack() as ctx:
+        const = ctx.enter_context(tc.tile_pool(name="const", bufs=1))
+        loaded = ctx.enter_context(tc.tile_pool(name="loaded", bufs=1))
+        work = ctx.enter_context(tc.tile_pool(name="work", bufs=3))
+        held = ctx.enter_context(tc.tile_pool(name="held", bufs=OUTPUT_LAG + 1))
+        packed = ctx.enter_context(tc.tile_pool(name="packed", bufs=OUTPUT_LAG - PACK_LAG + 2))
+        results = ctx.enter_context(tc.tile_pool(name="results", bufs=6))
+        transposed_psum = ctx.enter_context(tc.psum_pool(name="transposed_psum", bufs=1))
+        xw_psum = ctx.enter_context(tc.psum_pool(name="xw_psum", bufs=3))
+        sum_psum = ctx.enter_context(tc.psum_pool(name="sum_psum", bufs=2))
+        degree_psum = ctx.enter_context(tc.psum_pool(name="degree_psum", bufs=2))
+        ctx.enter_context(tc.manual_schedule())
+
+        raw = []
+        x_rows = []
+        x_view = x_gcn1.rearrange("g (p t) k -> p g t k", t=PACK)
+        w2_sb = const.tile([FEAT, WIDTH], BF16)
+        b2_row = const.tile([P, WIDTH], BF16)
+        nc.vector.memset(b2_row[:], 0.0)
+        nc.sync.dma_start(out=b2_row[0:1, :], in_=b2.rearrange("(o i) -> o i", o=1))
+        for q in range(GRAPHS // GROUP):
+            for g in range(q * GROUP, (q + 1) * GROUP):
+                raw_g = loaded.tile([P, PACK, NODES], BF16, name="raw%d" % g)
+                nc.sync.dma_start(out=raw_g[:], in_=flows[g].rearrange("(p j) c -> p j c", j=PACK))
+                raw.append(raw_g)
+            x_q = loaded.tile([P, GROUP, PACK, FEAT], BF16, name="x_rows%d" % q)
+            nc.sync.dma_start(out=x_q[:], in_=x_view[:, q * GROUP : (q + 1) * GROUP])
+            x_rows.append(x_q)
+            if q == 0:
+                nc.sync.dma_start(out=w2_sb[:], in_=W2)
+
+        one_column = const.tile([P, 1], F32)
+        nc.vector.memset(one_column[:], 1.0)
+        sqrt_of_one = const.tile([P, 1], F32)
+        nc.scalar.activation(out=sqrt_of_one[:], in_=one_column[:], func=ACT.Sqrt)
+
+        identity_bf16 = const.tile([P, P], BF16)
+        make_identity(nc, identity_bf16[:])
+        identity_f32 = const.tile([P, P], F32)
+        make_identity(nc, identity_f32[:])
+        ones_bf16 = const.tile([P, P], BF16)
+        nc.vector.memset(ones_bf16[:], 1.0)
+
+        lane_of = const.tile([P, PACK], F32)
+        nc.vector.tensor_reduce(
+            out=lane_of[:], in_=identity_f32[:].rearrange("p (m t) -> p t m", t=PACK), axis=AXIS.X, op=ALU.add
+        )
+        target = const.tile([P, PACK, P], F32)
+        nc.vector.memset(target[:], 0.0)
+        for b in range(PACK):
+            nc.vector.tensor_reduce(
+                out=target[:, b, b * QUARTER : (b + 1) * QUARTER],
+                in_=identity_f32[:].rearrange("p (m t) -> p m t", t=PACK),
+                axis=AXIS.X,
+                op=ALU.add,
+            )
+
+        b2_psum = xw_psum.tile([P, 2, WIDTH], F32, tag="xw")
+        nc.tensor.matmul(out=b2_psum[:, 0, :], lhsT=ones_bf16[:], rhs=b2_row[:], start=True, stop=True)
+        bias = const.tile([P, WIDTH], F32)
+        nc.vector.tensor_copy(out=bias[:], in_=b2_psum[:, 0, :])
+
+        degrees = {}
+        flows_grouped = {}
+        msg_grouped = {}
+        empty_nodes = {}
+        inverse_degrees = {}
+        roots = {}
+        dinv = {}
+        flow_codes = {}
+        flow_scales = {}
+        x_transposed_psum = {}
+        x_transposed = {}
+        xw = {}
+        msg_rows = {}
+        msg_codes = {}
+        msg_scales = {}
+        sums = {}
+
+        def add_up_degrees(g):
+            if g % GROUP == 0:
+                degree_tile = degree_psum.tile([P, 2, GROUP * PACK], F32)
+                degrees[g // GROUP] = degree_tile
+            by_block = degrees[g // GROUP][:, 0, :]
+            for b in range(PACK):
+                column = (g % GROUP) * PACK + b
+                for j in range(PACK):
+                    nc.tensor.matmul(
+                        out=by_block[:, column : column + 1],
+                        lhsT=raw[g][:, j, b * P : (b + 1) * P],
+                        rhs=ones_bf16[:, 0:1],
+                        start=(j == 0),
+                        stop=(j == PACK - 1),
+                    )
+
+        def regrouping_views(g):
+            to = flows_grouped[g][:].rearrange("p t m j -> p m j t")
+            source = raw[g][:].rearrange("p j (m t) -> p m j t", t=PACK)
+            return to, source
+
+        def regroup_flows_on_scalar(g):
+            grouped = work.tile([P, PACK, P, PACK], BF16, align_bytes=64, name="flows_grouped")
+            flows_grouped[g] = grouped
+            to, source = regrouping_views(g)
+            nc.scalar.copy(out=to[:, VECTOR_COLUMNS:], in_=source[:, VECTOR_COLUMNS:])
+
+        def regroup_flows_on_vector(g):
+            to, source = regrouping_views(g)
+            nc.vector.tensor_copy(out=to[:, :VECTOR_COLUMNS], in_=source[:, :VECTOR_COLUMNS])
+
+        def quantise_flows(g):
+            codes = held.tile([P, NODES], U32, align_bytes=64, name="flow_codes")
+            scales = held.tile([P, NODES], U8, align_bytes=64, name="flow_scales")
+            nc.vector.quantize_mx(
+                out=codes[:].bitcast(FP8X4), scales=scales[:], in_=flows_grouped[g][:].rearrange("p t m j -> p (t m j)")
+            )
+            flow_codes[g] = codes
+            flow_scales[g] = scales
+
+        def pick_lanes(q):
+            shape = [P, PACK, GROUP, PACK]
+            picked = work.tile(shape, F32)
+            nc.vector.tensor_tensor(
+                out=picked[:],
+                in0=degrees[q][:, 0, :].rearrange("p (i b) -> p b i", b=PACK).unsqueeze(3).to_broadcast(shape),
+                in1=lane_of[:].unsqueeze(1).unsqueeze(1).to_broadcast(shape),
+                op=ALU.mult,
+            )
+            return picked
+
+        def move_to_lanes(q, picked):
+            for b in range(PACK):
+                nc.tensor.matmul(
+                    out=degrees[q][:, 1, :],
+                    lhsT=target[:, b, :],
+                    rhs=picked[:, b].rearrange("p i t -> p (i t)"),
+                    start=(b == 0),
+                    stop=(b == PACK - 1),
+                )
+
+        def invert_degrees(q):
+            by_lane = degrees[q][:, 1, :]
+            empty = work.tile([P, GROUP * PACK], F32)
+            nc.vector.tensor_scalar(out=empty[:], in0=by_lane, scalar1=0.0, scalar2=None, op0=ALU.is_le)
+            safe = work.tile([P, GROUP * PACK], F32)
+            nc.vector.tensor_tensor(out=safe[:], in0=by_lane, in1=empty[:], op=ALU.add)
+            inverse = work.tile([P, GROUP * PACK], F32)
+            nc.vector.reciprocal(out=inverse[:], in_=safe[:])
+            empty_nodes[q] = empty
+            inverse_degrees[q] = inverse
+
+        def take_roots(q):
+            root = work.tile([P, GROUP * PACK], F32)
+            nc.scalar.activation(out=root[:], in_=inverse_degrees[q][:], func=ACT.Sqrt)
+            roots[q] = root
+
+        def zero_empty_nodes(q):
+            dinv_q = const.tile([P, GROUP * PACK], F32, name="dinv%d" % q)
+            nc.vector.scalar_tensor_tensor(
+                out=dinv_q[:], in0=empty_nodes[q][:], scalar=0.0, in1=roots[q][:], op0=ALU.is_equal, op1=ALU.mult
+            )
+            dinv[q] = dinv_q
+
+        def dinv_column(g, t):
+            column = (g % GROUP) * PACK + t
+            return dinv[g // GROUP][:, column : column + 1]
+
+        def transpose_x(g):
+            flipped = transposed_psum.tile([FEAT, PACK, P], BF16)
+            for t in range(PACK):
+                nc.tensor.transpose(
+                    out=flipped[:, t, :], in_=x_rows[g // GROUP][:, g % GROUP, t, :], identity=identity_bf16[:]
+                )
+            x_transposed_psum[g] = flipped
+
+        def copy_transposed_x(g):
+            copied = work.tile([FEAT, PACK, P], BF16, name="x_transposed")
+            nc.scalar.copy(out=copied[:], in_=x_transposed_psum[g][:])
+            x_transposed[g] = copied
+
+        def multiply_by_w2(g):
+            xw[g] = []
+            for half in range(2):
+                bank = xw_psum.tile([P, 2, WIDTH], F32, tag="xw", name="xw_bank")
+                for u in range(2):
+                    nc.tensor.matmul(
+                        out=bank[:, u, :], lhsT=x_transposed[g][:, 2 * half + u, :], rhs=w2_sb[:], start=True, stop=True
+                    )
+                xw[g].append(bank)
+
+        def scale_messages(g):
+            rows = work.tile([P, PACK, WIDTH], BF16, name="msg_rows")
+            for t in range(PACK):
+                nc.scalar.activation(
+                    out=rows[:, t, :], in_=xw[g][t // 2][:, t % 2, :], func=ACT.Copy, scale=dinv_column(g, t)
+                )
+            msg_rows[g] = rows
+
+        def regroup_messages(g):
+            grouped = work.tile([P, WIDTH, PACK], BF16, align_bytes=64, name="msg_grouped")
+            nc.vector.tensor_copy(
+                out=grouped[:].rearrange("p (c i) t -> p c t i", i=4),
+                in_=msg_rows[g][:].rearrange("p t (c i) -> p c t i", i=4),
+            )
+            msg_grouped[g] = grouped
+
+        def quantise_messages(g):
+            codes = packed.tile([P, WIDTH], U32, align_bytes=64, name="msg_codes")
+            scales = packed.tile([P, WIDTH], U8, align_bytes=64, name="msg_scales")
+            nc.vector.quantize_mx(
+                out=codes[:].bitcast(FP8X4), scales=scales[:], in_=msg_grouped[g][:].rearrange("p i t -> p (i t)")
+            )
+            msg_codes[g] = codes
+            msg_scales[g] = scales
+
+        def contract(g):
+            sums[g] = []
+            for half in range(2):
+                bank = sum_psum.tile([P, 2, WIDTH], F32, name="sum_bank")
+                for u in range(2):
+                    lane = slice((2 * half + u) * P, (2 * half + u + 1) * P)
+                    nc.tensor.matmul_mx(
+                        out=bank[:, u, :],
+                        lhsT=flow_codes[g][:, lane].bitcast(FP8X4),
+                        lhsT_scale=flow_scales[g][:, lane],
+                        rhs=msg_codes[g][:].bitcast(FP8X4),
+                        rhs_scale=msg_scales[g][:],
+                        start=True,
+                        stop=True,
+                    )
+                sums[g].append(bank)
+
+        def finish(g):
+            result = results.tile([P, PACK, WIDTH], F32)
+            for t in range(PACK):
+                nc.vector.scalar_tensor_tensor(
+                    out=result[:, t, :],
+                    in0=sums[g][t // 2][:, t % 2, :],
+                    scalar=dinv_column(g, t),
+                    in1=bias[:],
+                    op0=ALU.mult,
+                    op1=ALU.add,
+                )
+            nc.sync.dma_start(out=out[g].rearrange("(p t) i -> p t i", t=PACK), in_=result[:])
+
+        def graph_at(k, lag):
+            return k - lag if 0 <= k - lag < GRAPHS else None
+
+        def group_at(k, lag):
+            g = graph_at(k, lag)
+            return g // GROUP if g is not None and g % GROUP == GROUP - 1 else None
+
+        for k in range(GRAPHS + OUTPUT_LAG):
+            g_regroup = graph_at(k, 0)
+            g_quantise = graph_at(k, QUANTISE_LAG)
+            q_lanes = group_at(k, LANES_LAG)
+            q_root = group_at(k, ROOT_LAG)
+            g_transpose = graph_at(k, TRANSPOSE_LAG)
+            g_copy = graph_at(k, COPY_LAG)
+            g_message = graph_at(k, MESSAGE_LAG)
+            g_pack = graph_at(k, PACK_LAG)
+            g_output = graph_at(k, OUTPUT_LAG)
+
+            if g_regroup is not None:
+                regroup_flows_on_scalar(g_regroup)
+            if q_root is not None:
+                take_roots(q_root)
+            if g_copy is not None:
+                copy_transposed_x(g_copy)
+            if q_lanes is not None:
+                picked_degrees = pick_lanes(q_lanes)
+            if g_output is not None:
+                contract(g_output)
+            if g_transpose is not None:
+                transpose_x(g_transpose)
+            if g_message is not None:
+                multiply_by_w2(g_message)
+            if g_regroup is not None:
+                add_up_degrees(g_regroup)
+            if q_lanes is not None:
+                move_to_lanes(q_lanes, picked_degrees)
+            if g_message is not None:
+                scale_messages(g_message)
+            if g_quantise is not None:
+                quantise_flows(g_quantise)
+            if g_output is not None:
+                finish(g_output)
+            if g_pack is not None:
+                regroup_messages(g_pack)
+            if g_regroup is not None:
+                regroup_flows_on_vector(g_regroup)
+            if g_pack is not None:
+                quantise_messages(g_pack)
+            if q_lanes is not None:
+                invert_degrees(q_lanes)
+            if q_root is not None:
+                zero_empty_nodes(q_root)

@@ -134,12 +134,12 @@ def tile_encoder_flows_pb_t_kernel(tc, flows, x_gcn1, W2, b2, out):
                     )
 
         def regrouping_views(g):
-            to = flows_grouped[g][:].rearrange("p t m j -> p m j t")
-            source = raw[g][:].rearrange("p j (m t) -> p m j t", t=PACK)
+            to = flows_grouped[g][:].rearrange("p (m i) j -> p m j i", i=PACK)
+            source = raw[g][:].rearrange("p j (m i) -> p m j i", i=PACK)
             return to, source
 
         def regroup_flows_on_scalar(g):
-            grouped = work.tile([P, PACK, P, PACK], BF16, align_bytes=64, name="flows_grouped")
+            grouped = work.tile([P, NODES, PACK], BF16, align_bytes=64, name="flows_grouped")
             flows_grouped[g] = grouped
             to, source = regrouping_views(g)
             nc.scalar.copy(out=to[:, VECTOR_COLUMNS:], in_=source[:, VECTOR_COLUMNS:])
@@ -152,7 +152,7 @@ def tile_encoder_flows_pb_t_kernel(tc, flows, x_gcn1, W2, b2, out):
             codes = held.tile([P, NODES], U32, align_bytes=64, name="flow_codes")
             scales = held.tile([P, NODES], U8, align_bytes=64, name="flow_scales")
             nc.vector.quantize_mx(
-                out=codes[:].bitcast(FP8X4), scales=scales[:], in_=flows_grouped[g][:].rearrange("p t m j -> p (t m j)")
+                out=codes[:].bitcast(FP8X4), scales=scales[:], in_=flows_grouped[g][:].rearrange("p c j -> p (c j)")
             )
             flow_codes[g] = codes
             flow_scales[g] = scales
@@ -179,30 +179,34 @@ def tile_encoder_flows_pb_t_kernel(tc, flows, x_gcn1, W2, b2, out):
                 )
 
         def invert_degrees(q):
-            by_lane = degrees[q][:, 1, :]
-            empty = work.tile([P, GROUP * PACK], F32)
-            nc.vector.tensor_scalar(out=empty[:], in0=by_lane, scalar1=0.0, scalar2=None, op0=ALU.is_le)
-            safe = work.tile([P, GROUP * PACK], F32)
-            nc.vector.tensor_tensor(out=safe[:], in0=by_lane, in1=empty[:], op=ALU.add)
-            inverse = work.tile([P, GROUP * PACK], F32)
+            both = degrees[q][:].rearrange("p o c -> p (o c)")
+            empty = work.tile([P, 2 * GROUP * PACK], F32)
+            nc.vector.tensor_scalar(out=empty[:], in0=both, scalar1=0.0, scalar2=None, op0=ALU.is_le)
+            safe = work.tile([P, 2 * GROUP * PACK], F32)
+            nc.vector.tensor_tensor(out=safe[:], in0=both, in1=empty[:], op=ALU.add)
+            inverse = work.tile([P, 2 * GROUP * PACK], F32)
             nc.vector.reciprocal(out=inverse[:], in_=safe[:])
             empty_nodes[q] = empty
             inverse_degrees[q] = inverse
 
         def take_roots(q):
-            root = work.tile([P, GROUP * PACK], F32)
+            root = work.tile([P, 2 * GROUP * PACK], F32)
             nc.scalar.activation(out=root[:], in_=inverse_degrees[q][:], func=ACT.Sqrt)
             roots[q] = root
 
         def zero_empty_nodes(q):
-            dinv_q = const.tile([P, GROUP * PACK], F32, name="dinv%d" % q)
+            dinv_q = const.tile([P, 2 * GROUP * PACK], F32, name="dinv%d" % q)
             nc.vector.scalar_tensor_tensor(
                 out=dinv_q[:], in0=empty_nodes[q][:], scalar=0.0, in1=roots[q][:], op0=ALU.is_equal, op1=ALU.mult
             )
             dinv[q] = dinv_q
 
-        def dinv_column(g, t):
-            column = (g % GROUP) * PACK + t
+        def dinv_of_block(g, b):
+            column = (g % GROUP) * PACK + b
+            return dinv[g // GROUP][:, column : column + 1]
+
+        def dinv_of_lane(g, t):
+            column = (GROUP + g % GROUP) * PACK + t
             return dinv[g // GROUP][:, column : column + 1]
 
         def transpose_x(g):
@@ -232,7 +236,7 @@ def tile_encoder_flows_pb_t_kernel(tc, flows, x_gcn1, W2, b2, out):
             rows = work.tile([P, PACK, WIDTH], BF16, name="msg_rows")
             for t in range(PACK):
                 nc.scalar.activation(
-                    out=rows[:, t, :], in_=xw[g][t // 2][:, t % 2, :], func=ACT.Copy, scale=dinv_column(g, t)
+                    out=rows[:, t, :], in_=xw[g][t // 2][:, t % 2, :], func=ACT.Copy, scale=dinv_of_lane(g, t)
                 )
             msg_rows[g] = rows
 
@@ -276,12 +280,12 @@ def tile_encoder_flows_pb_t_kernel(tc, flows, x_gcn1, W2, b2, out):
                 nc.vector.scalar_tensor_tensor(
                     out=result[:, t, :],
                     in0=sums[g][t // 2][:, t % 2, :],
-                    scalar=dinv_column(g, t),
+                    scalar=dinv_of_block(g, t),
                     in1=bias[:],
                     op0=ALU.mult,
                     op1=ALU.add,
                 )
-            nc.sync.dma_start(out=out[g].rearrange("(p t) i -> p t i", t=PACK), in_=result[:])
+            nc.sync.dma_start(out=out[g].rearrange("(b p) i -> p b i", p=P), in_=result[:])
 
         def graph_at(k, lag):
             return k - lag if 0 <= k - lag < GRAPHS else None

@@ -134,12 +134,12 @@ def tile_encoder_flows_pb_t_kernel(tc, flows, x_gcn1, W2, b2, out):
                     )
 
         def regrouping_views(g):
-            to = flows_grouped[g][:].rearrange("p (m i) j -> p m j i", i=PACK)
-            source = raw[g][:].rearrange("p j (m i) -> p m j i", i=PACK)
+            to = flows_grouped[g][:].rearrange("p t m j -> p m j t")
+            source = raw[g][:].rearrange("p j (m t) -> p m j t", t=PACK)
             return to, source
 
         def regroup_flows_on_scalar(g):
-            grouped = work.tile([P, NODES, PACK], BF16, align_bytes=64, name="flows_grouped")
+            grouped = work.tile([P, PACK, P, PACK], BF16, align_bytes=64, name="flows_grouped")
             flows_grouped[g] = grouped
             to, source = regrouping_views(g)
             nc.scalar.copy(out=to[:, VECTOR_COLUMNS:], in_=source[:, VECTOR_COLUMNS:])
@@ -152,7 +152,7 @@ def tile_encoder_flows_pb_t_kernel(tc, flows, x_gcn1, W2, b2, out):
             codes = held.tile([P, NODES], U32, align_bytes=64, name="flow_codes")
             scales = held.tile([P, NODES], U8, align_bytes=64, name="flow_scales")
             nc.vector.quantize_mx(
-                out=codes[:].bitcast(FP8X4), scales=scales[:], in_=flows_grouped[g][:].rearrange("p c j -> p (c j)")
+                out=codes[:].bitcast(FP8X4), scales=scales[:], in_=flows_grouped[g][:].rearrange("p t m j -> p (t m j)")
             )
             flow_codes[g] = codes
             flow_scales[g] = scales
@@ -179,34 +179,30 @@ def tile_encoder_flows_pb_t_kernel(tc, flows, x_gcn1, W2, b2, out):
                 )
 
         def invert_degrees(q):
-            both = degrees[q][:].rearrange("p o c -> p (o c)")
-            empty = work.tile([P, 2 * GROUP * PACK], F32)
-            nc.vector.tensor_scalar(out=empty[:], in0=both, scalar1=0.0, scalar2=None, op0=ALU.is_le)
-            safe = work.tile([P, 2 * GROUP * PACK], F32)
-            nc.vector.tensor_tensor(out=safe[:], in0=both, in1=empty[:], op=ALU.add)
-            inverse = work.tile([P, 2 * GROUP * PACK], F32)
+            by_lane = degrees[q][:, 1, :]
+            empty = work.tile([P, GROUP * PACK], F32)
+            nc.vector.tensor_scalar(out=empty[:], in0=by_lane, scalar1=0.0, scalar2=None, op0=ALU.is_le)
+            safe = work.tile([P, GROUP * PACK], F32)
+            nc.vector.tensor_tensor(out=safe[:], in0=by_lane, in1=empty[:], op=ALU.add)
+            inverse = work.tile([P, GROUP * PACK], F32)
             nc.vector.reciprocal(out=inverse[:], in_=safe[:])
             empty_nodes[q] = empty
             inverse_degrees[q] = inverse
 
         def take_roots(q):
-            root = work.tile([P, 2 * GROUP * PACK], F32)
+            root = work.tile([P, GROUP * PACK], F32)
             nc.scalar.activation(out=root[:], in_=inverse_degrees[q][:], func=ACT.Sqrt)
             roots[q] = root
 
         def zero_empty_nodes(q):
-            dinv_q = const.tile([P, 2 * GROUP * PACK], F32, name="dinv%d" % q)
+            dinv_q = const.tile([P, GROUP * PACK], F32, name="dinv%d" % q)
             nc.vector.scalar_tensor_tensor(
                 out=dinv_q[:], in0=empty_nodes[q][:], scalar=0.0, in1=roots[q][:], op0=ALU.is_equal, op1=ALU.mult
             )
             dinv[q] = dinv_q
 
-        def dinv_of_block(g, b):
-            column = (g % GROUP) * PACK + b
-            return dinv[g // GROUP][:, column : column + 1]
-
-        def dinv_of_lane(g, t):
-            column = (GROUP + g % GROUP) * PACK + t
+        def dinv_column(g, t):
+            column = (g % GROUP) * PACK + t
             return dinv[g // GROUP][:, column : column + 1]
 
         def transpose_x(g):
@@ -236,7 +232,7 @@ def tile_encoder_flows_pb_t_kernel(tc, flows, x_gcn1, W2, b2, out):
             rows = work.tile([P, PACK, WIDTH], BF16, name="msg_rows")
             for t in range(PACK):
                 nc.scalar.activation(
-                    out=rows[:, t, :], in_=xw[g][t // 2][:, t % 2, :], func=ACT.Copy, scale=dinv_of_lane(g, t)
+                    out=rows[:, t, :], in_=xw[g][t // 2][:, t % 2, :], func=ACT.Copy, scale=dinv_column(g, t)
                 )
             msg_rows[g] = rows
 
@@ -280,12 +276,12 @@ def tile_encoder_flows_pb_t_kernel(tc, flows, x_gcn1, W2, b2, out):
                 nc.vector.scalar_tensor_tensor(
                     out=result[:, t, :],
                     in0=sums[g][t // 2][:, t % 2, :],
-                    scalar=dinv_of_block(g, t),
+                    scalar=dinv_column(g, t),
                     in1=bias[:],
                     op0=ALU.mult,
                     op1=ALU.add,
                 )
-            nc.sync.dma_start(out=out[g].rearrange("(b p) i -> p b i", p=P), in_=result[:])
+            nc.sync.dma_start(out=out[g].rearrange("(p t) i -> p t i", t=PACK), in_=result[:])
 
         def graph_at(k, lag):
             return k - lag if 0 <= k - lag < GRAPHS else None
@@ -315,14 +311,14 @@ def tile_encoder_flows_pb_t_kernel(tc, flows, x_gcn1, W2, b2, out):
                 picked_degrees = pick_lanes(q_lanes)
             if g_output is not None:
                 contract(g_output)
-            if g_transpose is not None:
-                transpose_x(g_transpose)
             if g_message is not None:
                 multiply_by_w2(g_message)
             if g_regroup is not None:
                 add_up_degrees(g_regroup)
             if q_lanes is not None:
                 move_to_lanes(q_lanes, picked_degrees)
+            if g_transpose is not None:
+                transpose_x(g_transpose)
             if g_message is not None:
                 scale_messages(g_message)
             if g_quantise is not None:

@@ -24,7 +24,8 @@ FLOPS = 2 * GRAPHS * NODES * FEAT * WIDTH + 2 * GRAPHS * NODES * NODES * WIDTH
 
 GROUP = 4
 
-VECTOR_COLUMNS = 48
+EARLY_COLUMNS = 80
+LATE_COLUMNS = 40
 
 QUANTISE_LAG = 1
 LANES_LAG = 1
@@ -33,7 +34,7 @@ TRANSPOSE_LAG = GROUP
 COPY_LAG = GROUP + 1
 MESSAGE_LAG = GROUP + 2
 PACK_LAG = GROUP + 3
-OUTPUT_LAG = GROUP + 5
+OUTPUT_LAG = GROUP + 4
 
 
 def tile_encoder_flows_pb_t_kernel(tc, flows, x_gcn1, W2, b2, out):
@@ -43,7 +44,7 @@ def tile_encoder_flows_pb_t_kernel(tc, flows, x_gcn1, W2, b2, out):
         loaded = ctx.enter_context(tc.tile_pool(name="loaded", bufs=1))
         work = ctx.enter_context(tc.tile_pool(name="work", bufs=3))
         held = ctx.enter_context(tc.tile_pool(name="held", bufs=OUTPUT_LAG + 1))
-        packed = ctx.enter_context(tc.tile_pool(name="packed", bufs=OUTPUT_LAG - PACK_LAG + 2))
+        packed = ctx.enter_context(tc.tile_pool(name="packed", bufs=3))
         results = ctx.enter_context(tc.tile_pool(name="results", bufs=6))
         transposed_psum = ctx.enter_context(tc.psum_pool(name="transposed_psum", bufs=1))
         xw_psum = ctx.enter_context(tc.psum_pool(name="xw_psum", bufs=3))
@@ -136,17 +137,18 @@ def tile_encoder_flows_pb_t_kernel(tc, flows, x_gcn1, W2, b2, out):
         def regrouping_views(g):
             to = flows_grouped[g][:].rearrange("p t m j -> p m j t")
             source = raw[g][:].rearrange("p j (m t) -> p m j t", t=PACK)
-            return to, source
+            vector_columns = EARLY_COLUMNS if g < OUTPUT_LAG else LATE_COLUMNS
+            return to, source, vector_columns
 
         def regroup_flows_on_scalar(g):
             grouped = work.tile([P, PACK, P, PACK], BF16, align_bytes=64, name="flows_grouped")
             flows_grouped[g] = grouped
-            to, source = regrouping_views(g)
-            nc.scalar.copy(out=to[:, VECTOR_COLUMNS:], in_=source[:, VECTOR_COLUMNS:])
+            to, source, vector_columns = regrouping_views(g)
+            nc.scalar.copy(out=to[:, vector_columns:], in_=source[:, vector_columns:])
 
         def regroup_flows_on_vector(g):
-            to, source = regrouping_views(g)
-            nc.vector.tensor_copy(out=to[:, :VECTOR_COLUMNS], in_=source[:, :VECTOR_COLUMNS])
+            to, source, vector_columns = regrouping_views(g)
+            nc.vector.tensor_copy(out=to[:, :vector_columns], in_=source[:, :vector_columns])
 
         def quantise_flows(g):
             codes = held.tile([P, NODES], U32, align_bytes=64, name="flow_codes")
@@ -310,9 +312,11 @@ def tile_encoder_flows_pb_t_kernel(tc, flows, x_gcn1, W2, b2, out):
             if q_lanes is not None:
                 picked_degrees = pick_lanes(q_lanes)
             if g_output is not None:
-                contract(g_output)
+                quantise_messages(g_output)
             if g_message is not None:
                 multiply_by_w2(g_message)
+            if g_output is not None:
+                contract(g_output)
             if g_regroup is not None:
                 add_up_degrees(g_regroup)
             if q_lanes is not None:
@@ -323,14 +327,12 @@ def tile_encoder_flows_pb_t_kernel(tc, flows, x_gcn1, W2, b2, out):
                 scale_messages(g_message)
             if g_quantise is not None:
                 quantise_flows(g_quantise)
-            if g_output is not None:
-                finish(g_output)
-            if g_pack is not None:
-                regroup_messages(g_pack)
             if g_regroup is not None:
                 regroup_flows_on_vector(g_regroup)
             if g_pack is not None:
-                quantise_messages(g_pack)
+                regroup_messages(g_pack)
+            if g_output is not None:
+                finish(g_output)
             if q_lanes is not None:
                 invert_degrees(q_lanes)
             if q_root is not None:

@@ -22,6 +22,8 @@ QUARTER = P // PACK
 
 FLOPS = 2 * GRAPHS * NODES * FEAT * WIDTH + 2 * GRAPHS * NODES * NODES * WIDTH
 
+FLOOR = 2.0**-86
+
 GROUP = 4
 
 EARLY_COLUMNS = 80
@@ -72,8 +74,10 @@ def tile_encoder_flows_pb_t_kernel(tc, flows, x_gcn1, W2, b2, out):
 
         one_column = const.tile([P, 1], F32)
         nc.vector.memset(one_column[:], 1.0)
-        sqrt_of_one = const.tile([P, 1], F32)
-        nc.scalar.activation(out=sqrt_of_one[:], in_=one_column[:], func=ACT.Sqrt)
+        root_of_one = const.tile([P, 1], F32)
+        nc.scalar.activation(out=root_of_one[:], in_=one_column[:], func=ACT.Abs_reciprocal_sqrt)
+        floor = const.tile([P, 1], F32)
+        nc.vector.memset(floor[:], FLOOR)
 
         identity_bf16 = const.tile([P, P], BF16)
         make_identity(nc, identity_bf16[:])
@@ -104,8 +108,6 @@ def tile_encoder_flows_pb_t_kernel(tc, flows, x_gcn1, W2, b2, out):
         degrees = {}
         flows_grouped = {}
         msg_grouped = {}
-        empty_nodes = {}
-        inverse_degrees = {}
         roots = {}
         dinv = {}
         flow_codes = {}
@@ -180,26 +182,17 @@ def tile_encoder_flows_pb_t_kernel(tc, flows, x_gcn1, W2, b2, out):
                     stop=(b == PACK - 1),
                 )
 
-        def invert_degrees(q):
-            by_lane = degrees[q][:, 1, :]
-            empty = work.tile([P, GROUP * PACK], F32)
-            nc.vector.tensor_scalar(out=empty[:], in0=by_lane, scalar1=0.0, scalar2=None, op0=ALU.is_le)
-            safe = work.tile([P, GROUP * PACK], F32)
-            nc.vector.tensor_tensor(out=safe[:], in0=by_lane, in1=empty[:], op=ALU.add)
-            inverse = work.tile([P, GROUP * PACK], F32)
-            nc.vector.reciprocal(out=inverse[:], in_=safe[:])
-            empty_nodes[q] = empty
-            inverse_degrees[q] = inverse
-
-        def take_roots(q):
-            root = work.tile([P, GROUP * PACK], F32)
-            nc.scalar.activation(out=root[:], in_=inverse_degrees[q][:], func=ACT.Sqrt)
+        def take_inverse_roots(q):
+            root = work.tile([P, GROUP * PACK], F32, name="inverse_root")
+            nc.scalar.activation(
+                out=root[:], in_=degrees[q][:, 1, :], func=ACT.Abs_reciprocal_sqrt, bias=floor[:]
+            )
             roots[q] = root
 
         def zero_empty_nodes(q):
             dinv_q = const.tile([P, GROUP * PACK], F32, name="dinv%d" % q)
             nc.vector.scalar_tensor_tensor(
-                out=dinv_q[:], in0=empty_nodes[q][:], scalar=0.0, in1=roots[q][:], op0=ALU.is_equal, op1=ALU.mult
+                out=dinv_q[:], in0=degrees[q][:, 1, :], scalar=0.0, in1=roots[q][:], op0=ALU.is_gt, op1=ALU.mult
             )
             dinv[q] = dinv_q
 
@@ -306,7 +299,7 @@ def tile_encoder_flows_pb_t_kernel(tc, flows, x_gcn1, W2, b2, out):
             if g_regroup is not None:
                 regroup_flows_on_scalar(g_regroup)
             if q_root is not None:
-                take_roots(q_root)
+                take_inverse_roots(q_root)
             if g_copy is not None:
                 copy_transposed_x(g_copy)
             if q_lanes is not None:
@@ -333,7 +326,5 @@ def tile_encoder_flows_pb_t_kernel(tc, flows, x_gcn1, W2, b2, out):
                 regroup_messages(g_pack)
             if g_output is not None:
                 finish(g_output)
-            if q_lanes is not None:
-                invert_degrees(q_lanes)
             if q_root is not None:
                 zero_empty_nodes(q_root)

@@ -265,6 +265,9 @@ def tile_encoder_flows_pb_t_kernel(tc, flows, x_gcn1, W2, b2, out):
                     )
                 sums[g].append(bank)
 
+        def store(g, result, lanes):
+            nc.sync.dma_start(out=out[g].rearrange("(p t) i -> p t i", t=PACK)[:, lanes], in_=result[:, lanes])
+
         def finish(g):
             result = results.tile([P, PACK, WIDTH], F32)
             for t in range(PACK):
@@ -276,7 +279,10 @@ def tile_encoder_flows_pb_t_kernel(tc, flows, x_gcn1, W2, b2, out):
                     op0=ALU.mult,
                     op1=ALU.add,
                 )
-            nc.sync.dma_start(out=out[g].rearrange("(p t) i -> p t i", t=PACK), in_=result[:])
+                if g == GRAPHS - 1 and t % 2 == 1:
+                    store(g, result, slice(t - 1, t + 1))
+            if g < GRAPHS - 1:
+                store(g, result, slice(0, PACK))
 
         def graph_at(k, lag):
             return k - lag if 0 <= k - lag < GRAPHS else None
@@ -302,10 +308,12 @@ def tile_encoder_flows_pb_t_kernel(tc, flows, x_gcn1, W2, b2, out):
                 take_inverse_roots(q_root)
             if g_copy is not None:
                 copy_transposed_x(g_copy)
-            if q_lanes is not None:
-                picked_degrees = pick_lanes(q_lanes)
             if g_output is not None:
                 quantise_messages(g_output)
+            if g_quantise is not None:
+                quantise_flows(g_quantise)
+            if q_lanes is not None:
+                picked_degrees = pick_lanes(q_lanes)
             if g_message is not None:
                 multiply_by_w2(g_message)
             if g_output is not None:
@@ -318,8 +326,6 @@ def tile_encoder_flows_pb_t_kernel(tc, flows, x_gcn1, W2, b2, out):
                 transpose_x(g_transpose)
             if g_message is not None:
                 scale_messages(g_message)
-            if g_quantise is not None:
-                quantise_flows(g_quantise)
             if g_regroup is not None:
                 regroup_flows_on_vector(g_regroup)
             if g_pack is not None:

@@ -26,8 +26,10 @@ FLOOR = 2.0**-86
 
 GROUP = 4
 
-EARLY_COLUMNS = 80
+EARLY_COLUMNS = 64
+MIDDLE_COLUMNS = 96
 LATE_COLUMNS = 40
+SCALAR_GROUPS = 16
 
 QUANTISE_LAG = 1
 LANES_LAG = 1
@@ -61,15 +63,16 @@ def tile_encoder_flows_pb_t_kernel(tc, flows, x_gcn1, W2, b2, out):
         b2_row = const.tile([P, WIDTH], BF16)
         nc.vector.memset(b2_row[:], 0.0)
         nc.sync.dma_start(out=b2_row[0:1, :], in_=b2.rearrange("(o i) -> o i", o=1))
-        for q in range(GRAPHS // GROUP):
-            for g in range(q * GROUP, (q + 1) * GROUP):
-                raw_g = loaded.tile([P, PACK, NODES], BF16, name="raw%d" % g)
-                nc.sync.dma_start(out=raw_g[:], in_=flows[g].rearrange("(p j) c -> p j c", j=PACK))
-                raw.append(raw_g)
-            x_q = loaded.tile([P, GROUP, PACK, FEAT], BF16, name="x_rows%d" % q)
-            nc.sync.dma_start(out=x_q[:], in_=x_view[:, q * GROUP : (q + 1) * GROUP])
-            x_rows.append(x_q)
-            if q == 0:
+        for g in range(GRAPHS):
+            raw_g = loaded.tile([P, PACK, NODES], BF16, name="raw%d" % g)
+            nc.sync.dma_start(out=raw_g[:], in_=flows[g].rearrange("(p j) c -> p j c", j=PACK))
+            raw.append(raw_g)
+            if g % GROUP == 0 and g > 0 or g == GRAPHS - 1:
+                q = len(x_rows)
+                x_q = loaded.tile([P, GROUP, PACK, FEAT], BF16, name="x_rows%d" % q)
+                nc.sync.dma_start(out=x_q[:], in_=x_view[:, q * GROUP : (q + 1) * GROUP])
+                x_rows.append(x_q)
+            if g == GROUP:
                 nc.sync.dma_start(out=w2_sb[:], in_=W2)
 
         one_column = const.tile([P, 1], F32)
@@ -139,7 +142,12 @@ def tile_encoder_flows_pb_t_kernel(tc, flows, x_gcn1, W2, b2, out):
         def regrouping_views(g):
             to = flows_grouped[g][:].rearrange("p t m j -> p m j t")
             source = raw[g][:].rearrange("p j (m t) -> p m j t", t=PACK)
-            vector_columns = EARLY_COLUMNS if g < OUTPUT_LAG else LATE_COLUMNS
+            if g < MESSAGE_LAG:
+                vector_columns = EARLY_COLUMNS
+            elif g < OUTPUT_LAG:
+                vector_columns = MIDDLE_COLUMNS
+            else:
+                vector_columns = LATE_COLUMNS
             return to, source, vector_columns
 
         def regroup_flows_on_scalar(g):
@@ -233,10 +241,13 @@ def tile_encoder_flows_pb_t_kernel(tc, flows, x_gcn1, W2, b2, out):
 
         def regroup_messages(g):
             grouped = work.tile([P, WIDTH, PACK], BF16, align_bytes=64, name="msg_grouped")
-            nc.vector.tensor_copy(
-                out=grouped[:].rearrange("p (c i) t -> p c t i", i=4),
-                in_=msg_rows[g][:].rearrange("p t (c i) -> p c t i", i=4),
-            )
+            to = grouped[:].rearrange("p (c i) t -> p c t i", i=4)
+            source = msg_rows[g][:].rearrange("p t (c i) -> p c t i", i=4)
+            scalar_groups = SCALAR_GROUPS if g + PACK_LAG >= GRAPHS else 0
+            vector_groups = WIDTH // 4 - scalar_groups
+            nc.vector.tensor_copy(out=to[:, :vector_groups], in_=source[:, :vector_groups])
+            if scalar_groups > 0:
+                nc.scalar.copy(out=to[:, vector_groups:], in_=source[:, vector_groups:])
             msg_grouped[g] = grouped
 
         def quantise_messages(g):
@@ -310,9 +321,11 @@ def tile_encoder_flows_pb_t_kernel(tc, flows, x_gcn1, W2, b2, out):
                 copy_transposed_x(g_copy)
             if g_output is not None:
                 quantise_messages(g_output)
+            if q_lanes == 0:
+                picked_degrees = pick_lanes(q_lanes)
             if g_quantise is not None:
                 quantise_flows(g_quantise)
-            if q_lanes is not None:
+            if q_lanes is not None and q_lanes > 0:
                 picked_degrees = pick_lanes(q_lanes)
             if g_message is not None:
                 multiply_by_w2(g_message)

@@ -30,6 +30,10 @@ EARLY_COLUMNS = 64
 MIDDLE_COLUMNS = 96
 LATE_COLUMNS = 40
 SCALAR_GROUPS = 16
+LAST_SCALAR_GROUPS = 32
+
+PAIR = 2
+FLOWS_AHEAD = 4
 
 QUANTISE_LAG = 1
 LANES_LAG = 1
@@ -62,18 +66,17 @@ def tile_encoder_flows_pb_t_kernel(tc, flows, x_gcn1, W2, b2, out):
         w2_sb = const.tile([FEAT, WIDTH], BF16)
         b2_row = const.tile([P, WIDTH], BF16)
         nc.vector.memset(b2_row[:], 0.0)
-        nc.sync.dma_start(out=b2_row[0:1, :], in_=b2.rearrange("(o i) -> o i", o=1))
+        nc.scalar.dma_start(out=b2_row[0:1, :], in_=b2.rearrange("(o i) -> o i", o=1))
+        nc.scalar.dma_start(out=w2_sb[:], in_=W2)
         for g in range(GRAPHS):
             raw_g = loaded.tile([P, PACK, NODES], BF16, name="raw%d" % g)
             nc.sync.dma_start(out=raw_g[:], in_=flows[g].rearrange("(p j) c -> p j c", j=PACK))
             raw.append(raw_g)
-            if g % GROUP == 0 and g > 0 or g == GRAPHS - 1:
-                q = len(x_rows)
-                x_q = loaded.tile([P, GROUP, PACK, FEAT], BF16, name="x_rows%d" % q)
-                nc.sync.dma_start(out=x_q[:], in_=x_view[:, q * GROUP : (q + 1) * GROUP])
-                x_rows.append(x_q)
-            if g == GROUP:
-                nc.sync.dma_start(out=w2_sb[:], in_=W2)
+            for q in range(GRAPHS // PAIR):
+                if g == min(PAIR * (q + 1) - 1 + FLOWS_AHEAD, GRAPHS - 1):
+                    x_q = loaded.tile([P, PAIR, PACK, FEAT], BF16, name="x_rows%d" % q)
+                    nc.sync.dma_start(out=x_q[:], in_=x_view[:, q * PAIR : (q + 1) * PAIR])
+                    x_rows.append(x_q)
 
         one_column = const.tile([P, 1], F32)
         nc.vector.memset(one_column[:], 1.0)
@@ -212,7 +215,7 @@ def tile_encoder_flows_pb_t_kernel(tc, flows, x_gcn1, W2, b2, out):
             flipped = transposed_psum.tile([FEAT, PACK, P], BF16)
             for t in range(PACK):
                 nc.tensor.transpose(
-                    out=flipped[:, t, :], in_=x_rows[g // GROUP][:, g % GROUP, t, :], identity=identity_bf16[:]
+                    out=flipped[:, t, :], in_=x_rows[g // PAIR][:, g % PAIR, t, :], identity=identity_bf16[:]
                 )
             x_transposed_psum[g] = flipped
 
@@ -243,7 +246,9 @@ def tile_encoder_flows_pb_t_kernel(tc, flows, x_gcn1, W2, b2, out):
             grouped = work.tile([P, WIDTH, PACK], BF16, align_bytes=64, name="msg_grouped")
             to = grouped[:].rearrange("p (c i) t -> p c t i", i=4)
             source = msg_rows[g][:].rearrange("p t (c i) -> p c t i", i=4)
-            scalar_groups = SCALAR_GROUPS if g + PACK_LAG >= GRAPHS else 0
+            scalar_groups = 0
+            if g + PACK_LAG >= GRAPHS:
+                scalar_groups = SCALAR_GROUPS if g < GRAPHS - 1 else LAST_SCALAR_GROUPS
             vector_groups = WIDTH // 4 - scalar_groups
             nc.vector.tensor_copy(out=to[:, :vector_groups], in_=source[:, :vector_groups])
             if scalar_groups > 0:
@@ -313,10 +318,10 @@ def tile_encoder_flows_pb_t_kernel(tc, flows, x_gcn1, W2, b2, out):
             g_pack = graph_at(k, PACK_LAG)
             g_output = graph_at(k, OUTPUT_LAG)
 
-            if g_regroup is not None:
-                regroup_flows_on_scalar(g_regroup)
             if q_root is not None:
                 take_inverse_roots(q_root)
+            if g_regroup is not None:
+                regroup_flows_on_scalar(g_regroup)
             if g_copy is not None:
                 copy_transposed_x(g_copy)
             if g_output is not None:

@@ -13,6 +13,7 @@ ACT = mybir.ActivationFunctionType
 AXIS = mybir.AxisListType
 
 GRAPHS = 16
+LAST = GRAPHS - 1
 NODES = 512
 FEAT = 128
 WIDTH = 256
@@ -30,7 +31,6 @@ EARLY_COLUMNS = 64
 MIDDLE_COLUMNS = 96
 LATE_COLUMNS = 40
 SCALAR_GROUPS = 16
-LAST_SCALAR_GROUPS = 32
 
 PAIR = 2
 FLOWS_AHEAD = 4
@@ -66,12 +66,13 @@ def tile_encoder_flows_pb_t_kernel(tc, flows, x_gcn1, W2, b2, out):
         w2_sb = const.tile([FEAT, WIDTH], BF16)
         b2_row = const.tile([P, WIDTH], BF16)
         nc.vector.memset(b2_row[:], 0.0)
-        nc.scalar.dma_start(out=b2_row[0:1, :], in_=b2.rearrange("(o i) -> o i", o=1))
-        nc.scalar.dma_start(out=w2_sb[:], in_=W2)
         for g in range(GRAPHS):
             raw_g = loaded.tile([P, PACK, NODES], BF16, name="raw%d" % g)
             nc.sync.dma_start(out=raw_g[:], in_=flows[g].rearrange("(p j) c -> p j c", j=PACK))
             raw.append(raw_g)
+            if g == 0:
+                nc.sync.dma_start(out=b2_row[0:1, :], in_=b2.rearrange("(o i) -> o i", o=1))
+                nc.sync.dma_start(out=w2_sb[:], in_=W2)
             for q in range(GRAPHS // PAIR):
                 if g == min(PAIR * (q + 1) - 1 + FLOWS_AHEAD, GRAPHS - 1):
                     x_q = loaded.tile([P, PAIR, PACK, FEAT], BF16, name="x_rows%d" % q)
@@ -106,10 +107,12 @@ def tile_encoder_flows_pb_t_kernel(tc, flows, x_gcn1, W2, b2, out):
                 op=ALU.add,
             )
 
-        b2_psum = xw_psum.tile([P, 2, WIDTH], F32, tag="xw")
-        nc.tensor.matmul(out=b2_psum[:, 0, :], lhsT=ones_bf16[:], rhs=b2_row[:], start=True, stop=True)
         bias = const.tile([P, WIDTH], F32)
-        nc.vector.tensor_copy(out=bias[:], in_=b2_psum[:, 0, :])
+
+        def spread_bias():
+            spread = xw_psum.tile([P, 2, WIDTH], F32, tag="xw", name="spread_bias")
+            nc.tensor.matmul(out=spread[:, 0, :], lhsT=ones_bf16[:], rhs=b2_row[:], start=True, stop=True)
+            nc.vector.tensor_copy(out=bias[:], in_=spread[:, 0, :])
 
         degrees = {}
         flows_grouped = {}
@@ -246,12 +249,15 @@ def tile_encoder_flows_pb_t_kernel(tc, flows, x_gcn1, W2, b2, out):
             grouped = work.tile([P, WIDTH, PACK], BF16, align_bytes=64, name="msg_grouped")
             to = grouped[:].rearrange("p (c i) t -> p c t i", i=4)
             source = msg_rows[g][:].rearrange("p t (c i) -> p c t i", i=4)
-            scalar_groups = 0
-            if g + PACK_LAG >= GRAPHS:
-                scalar_groups = SCALAR_GROUPS if g < GRAPHS - 1 else LAST_SCALAR_GROUPS
-            vector_groups = WIDTH // 4 - scalar_groups
-            nc.vector.tensor_copy(out=to[:, :vector_groups], in_=source[:, :vector_groups])
-            if scalar_groups > 0:
+            if g == LAST:
+                vector_groups = 0
+            elif g + PACK_LAG >= GRAPHS:
+                vector_groups = WIDTH // 4 - SCALAR_GROUPS
+            else:
+                vector_groups = WIDTH // 4
+            if vector_groups > 0:
+                nc.vector.tensor_copy(out=to[:, :vector_groups], in_=source[:, :vector_groups])
+            if vector_groups < WIDTH // 4:
                 nc.scalar.copy(out=to[:, vector_groups:], in_=source[:, vector_groups:])
             msg_grouped[g] = grouped
 
@@ -281,9 +287,6 @@ def tile_encoder_flows_pb_t_kernel(tc, flows, x_gcn1, W2, b2, out):
                     )
                 sums[g].append(bank)
 
-        def store(g, result, lanes):
-            nc.sync.dma_start(out=out[g].rearrange("(p t) i -> p t i", t=PACK)[:, lanes], in_=result[:, lanes])
-
         def finish(g):
             result = results.tile([P, PACK, WIDTH], F32)
             for t in range(PACK):
@@ -295,10 +298,9 @@ def tile_encoder_flows_pb_t_kernel(tc, flows, x_gcn1, W2, b2, out):
                     op0=ALU.mult,
                     op1=ALU.add,
                 )
-                if g == GRAPHS - 1 and t % 2 == 1:
-                    store(g, result, slice(t - 1, t + 1))
-            if g < GRAPHS - 1:
-                store(g, result, slice(0, PACK))
+                if t % 2 == 1:
+                    lanes = slice(t - 1, t + 1)
+                    nc.sync.dma_start(out=out[g].rearrange("(p t) i -> p t i", t=PACK)[:, lanes], in_=result[:, lanes])
 
         def graph_at(k, lag):
             return k - lag if 0 <= k - lag < GRAPHS else None
@@ -318,14 +320,20 @@ def tile_encoder_flows_pb_t_kernel(tc, flows, x_gcn1, W2, b2, out):
             g_pack = graph_at(k, PACK_LAG)
             g_output = graph_at(k, OUTPUT_LAG)
 
-            if q_root is not None:
-                take_inverse_roots(q_root)
+            if k == 1:
+                spread_bias()
             if g_regroup is not None:
                 regroup_flows_on_scalar(g_regroup)
             if g_copy is not None:
                 copy_transposed_x(g_copy)
-            if g_output is not None:
+            if q_root is not None:
+                take_inverse_roots(q_root)
+            if g_pack == LAST:
+                regroup_messages(LAST)
+            if g_output is not None and g_output != LAST:
                 quantise_messages(g_output)
+            if g_pack == LAST:
+                quantise_messages(LAST)
             if q_lanes == 0:
                 picked_degrees = pick_lanes(q_lanes)
             if g_quantise is not None:
@@ -346,7 +354,7 @@ def tile_encoder_flows_pb_t_kernel(tc, flows, x_gcn1, W2, b2, out):
                 scale_messages(g_message)
             if g_regroup is not None:
                 regroup_flows_on_vector(g_regroup)
-            if g_pack is not None:
+            if g_pack is not None and g_pack != LAST:
                 regroup_messages(g_pack)
             if g_output is not None:
                 finish(g_output)

@@ -10,7 +10,6 @@ U8 = mybir.dt.uint8
 FP8X4 = mybir.dt.float8_e4m3fn_x4
 ALU = mybir.AluOpType
 ACT = mybir.ActivationFunctionType
-AXIS = mybir.AxisListType
 
 GRAPHS = 16
 LAST = GRAPHS - 1
@@ -19,7 +18,6 @@ FEAT = 128
 WIDTH = 256
 P = 128
 PACK = 4
-QUARTER = P // PACK
 
 FLOPS = 2 * GRAPHS * NODES * FEAT * WIDTH + 2 * GRAPHS * NODES * NODES * WIDTH
 
@@ -36,8 +34,7 @@ PAIR = 2
 FLOWS_AHEAD = 4
 
 QUANTISE_LAG = 1
-LANES_LAG = 1
-ROOT_LAG = 2
+ROOT_LAG = 1
 TRANSPOSE_LAG = GROUP
 COPY_LAG = GROUP + 1
 MESSAGE_LAG = GROUP + 2
@@ -88,24 +85,8 @@ def tile_encoder_flows_pb_t_kernel(tc, flows, x_gcn1, W2, b2, out):
 
         identity_bf16 = const.tile([P, P], BF16)
         make_identity(nc, identity_bf16[:])
-        identity_f32 = const.tile([P, P], F32)
-        make_identity(nc, identity_f32[:])
         ones_bf16 = const.tile([P, P], BF16)
         nc.vector.memset(ones_bf16[:], 1.0)
-
-        lane_of = const.tile([P, PACK], F32)
-        nc.vector.tensor_reduce(
-            out=lane_of[:], in_=identity_f32[:].rearrange("p (m t) -> p t m", t=PACK), axis=AXIS.X, op=ALU.add
-        )
-        target = const.tile([P, PACK, P], F32)
-        nc.vector.memset(target[:], 0.0)
-        for b in range(PACK):
-            nc.vector.tensor_reduce(
-                out=target[:, b, b * QUARTER : (b + 1) * QUARTER],
-                in_=identity_f32[:].rearrange("p (m t) -> p m t", t=PACK),
-                axis=AXIS.X,
-                op=ALU.add,
-            )
 
         bias = const.tile([P, WIDTH], F32)
 
@@ -131,15 +112,14 @@ def tile_encoder_flows_pb_t_kernel(tc, flows, x_gcn1, W2, b2, out):
 
         def add_up_degrees(g):
             if g % GROUP == 0:
-                degree_tile = degree_psum.tile([P, 2, GROUP * PACK], F32)
+                degree_tile = degree_psum.tile([P, GROUP * PACK], F32)
                 degrees[g // GROUP] = degree_tile
-            by_block = degrees[g // GROUP][:, 0, :]
-            for b in range(PACK):
-                column = (g % GROUP) * PACK + b
+            for t in range(PACK):
+                column = (g % GROUP) * PACK + t
                 for j in range(PACK):
                     nc.tensor.matmul(
-                        out=by_block[:, column : column + 1],
-                        lhsT=raw[g][:, j, b * P : (b + 1) * P],
+                        out=degrees[g // GROUP][:, column : column + 1],
+                        lhsT=raw[g][:, j, t :: PACK],
                         rhs=ones_bf16[:, 0:1],
                         start=(j == 0),
                         stop=(j == PACK - 1),
@@ -175,38 +155,17 @@ def tile_encoder_flows_pb_t_kernel(tc, flows, x_gcn1, W2, b2, out):
             flow_codes[g] = codes
             flow_scales[g] = scales
 
-        def pick_lanes(q):
-            shape = [P, PACK, GROUP, PACK]
-            picked = work.tile(shape, F32)
-            nc.vector.tensor_tensor(
-                out=picked[:],
-                in0=degrees[q][:, 0, :].rearrange("p (i b) -> p b i", b=PACK).unsqueeze(3).to_broadcast(shape),
-                in1=lane_of[:].unsqueeze(1).unsqueeze(1).to_broadcast(shape),
-                op=ALU.mult,
-            )
-            return picked
-
-        def move_to_lanes(q, picked):
-            for b in range(PACK):
-                nc.tensor.matmul(
-                    out=degrees[q][:, 1, :],
-                    lhsT=target[:, b, :],
-                    rhs=picked[:, b].rearrange("p i t -> p (i t)"),
-                    start=(b == 0),
-                    stop=(b == PACK - 1),
-                )
-
         def take_inverse_roots(q):
             root = work.tile([P, GROUP * PACK], F32, name="inverse_root")
             nc.scalar.activation(
-                out=root[:], in_=degrees[q][:, 1, :], func=ACT.Abs_reciprocal_sqrt, bias=floor[:]
+                out=root[:], in_=degrees[q][:], func=ACT.Abs_reciprocal_sqrt, bias=floor[:]
             )
             roots[q] = root
 
         def zero_empty_nodes(q):
             dinv_q = const.tile([P, GROUP * PACK], F32, name="dinv%d" % q)
             nc.vector.scalar_tensor_tensor(
-                out=dinv_q[:], in0=degrees[q][:, 1, :], scalar=0.0, in1=roots[q][:], op0=ALU.is_gt, op1=ALU.mult
+                out=dinv_q[:], in0=degrees[q][:], scalar=0.0, in1=roots[q][:], op0=ALU.is_gt, op1=ALU.mult
             )
             dinv[q] = dinv_q
 
@@ -312,7 +271,6 @@ def tile_encoder_flows_pb_t_kernel(tc, flows, x_gcn1, W2, b2, out):
         for k in range(GRAPHS + OUTPUT_LAG):
             g_regroup = graph_at(k, 0)
             g_quantise = graph_at(k, QUANTISE_LAG)
-            q_lanes = group_at(k, LANES_LAG)
             q_root = group_at(k, ROOT_LAG)
             g_transpose = graph_at(k, TRANSPOSE_LAG)
             g_copy = graph_at(k, COPY_LAG)
@@ -334,20 +292,14 @@ def tile_encoder_flows_pb_t_kernel(tc, flows, x_gcn1, W2, b2, out):
                 quantise_messages(g_output)
             if g_pack == LAST:
                 quantise_messages(LAST)
-            if q_lanes == 0:
-                picked_degrees = pick_lanes(q_lanes)
             if g_quantise is not None:
                 quantise_flows(g_quantise)
-            if q_lanes is not None and q_lanes > 0:
-                picked_degrees = pick_lanes(q_lanes)
             if g_message is not None:
                 multiply_by_w2(g_message)
             if g_output is not None:
                 contract(g_output)
             if g_regroup is not None:
                 add_up_degrees(g_regroup)
-            if q_lanes is not None:
-                move_to_lanes(q_lanes, picked_degrees)
             if g_transpose is not None:
                 transpose_x(g_transpose)
             if g_message is not None:

@@ -23,15 +23,15 @@ FLOPS = 2 * GRAPHS * NODES * FEAT * WIDTH + 2 * GRAPHS * NODES * NODES * WIDTH
 
 FLOOR = 2.0**-86
 
-GROUP = 4
+GROUP = 2
 
 EARLY_COLUMNS = 64
 MIDDLE_COLUMNS = 96
-LATE_COLUMNS = 40
+LATE_COLUMNS = 48
 SCALAR_GROUPS = 16
 
 PAIR = 2
-FLOWS_AHEAD = 4
+FLOWS_AHEAD = 2
 
 QUANTISE_LAG = 1
 ROOT_LAG = 1

@@ -23,14 +23,14 @@ FLOPS = 2 * GRAPHS * NODES * FEAT * WIDTH + 2 * GRAPHS * NODES * NODES * WIDTH
 
 FLOOR = 2.0**-86
 
-GROUP = 2
+GROUP = 1
 
-EARLY_COLUMNS = 64
-MIDDLE_COLUMNS = 96
+EARLY_COLUMNS = 80
+MIDDLE_COLUMNS = 112
 LATE_COLUMNS = 48
 SCALAR_GROUPS = 16
 
-PAIR = 2
+PAIR = 1
 FLOWS_AHEAD = 2
 
 QUANTISE_LAG = 1

@@ -27,7 +27,8 @@ GROUP = 1
 
 EARLY_COLUMNS = 80
 MIDDLE_COLUMNS = 112
-LATE_COLUMNS = 48
+LATE_COLUMNS = 32
+GPSIMD_COLUMNS = 16
 SCALAR_GROUPS = 16
 
 PAIR = 1
@@ -134,16 +135,25 @@ def tile_encoder_flows_pb_t_kernel(tc, flows, x_gcn1, W2, b2, out):
                 vector_columns = MIDDLE_COLUMNS
             else:
                 vector_columns = LATE_COLUMNS
-            return to, source, vector_columns
+            return to, source, vector_columns, vector_columns + (GPSIMD_COLUMNS if g >= OUTPUT_LAG else 0)
 
         def regroup_flows_on_scalar(g):
             grouped = work.tile([P, PACK, P, PACK], BF16, align_bytes=64, name="flows_grouped")
             flows_grouped[g] = grouped
-            to, source, vector_columns = regrouping_views(g)
-            nc.scalar.copy(out=to[:, vector_columns:], in_=source[:, vector_columns:])
+            to, source, vector_columns, first = regrouping_views(g)
+            nc.scalar.copy(out=to[:, first:], in_=source[:, first:])
+            if first > vector_columns:
+                nc.gpsimd.tensor_scalar(
+                    out=to[:, vector_columns:first],
+                    in0=source[:, vector_columns:first],
+                    scalar1=1.0,
+                    scalar2=0.0,
+                    op0=ALU.mult,
+                    op1=ALU.add,
+                )
 
         def regroup_flows_on_vector(g):
-            to, source, vector_columns = regrouping_views(g)
+            to, source, vector_columns, first = regrouping_views(g)
             nc.vector.tensor_copy(out=to[:, :vector_columns], in_=source[:, :vector_columns])
 
         def quantise_flows(g):

from contextlib import ExitStack

import concourse.mybir as mybir
from concourse.masks import make_identity

F32 = mybir.dt.float32
BF16 = mybir.dt.bfloat16
U32 = mybir.dt.uint32
U8 = mybir.dt.uint8
FP8X4 = mybir.dt.float8_e4m3fn_x4
ALU = mybir.AluOpType
ACT = mybir.ActivationFunctionType

GRAPHS = 16
LAST = GRAPHS - 1
NODES = 512
FEAT = 128
WIDTH = 256
P = 128
PACK = 4

FLOPS = 2 * GRAPHS * NODES * FEAT * WIDTH + 2 * GRAPHS * NODES * NODES * WIDTH

FLOOR = 2.0**-86

GROUP = 1

EARLY_COLUMNS = 80
MIDDLE_COLUMNS = 112
LATE_COLUMNS = 32
GPSIMD_COLUMNS = 16
SCALAR_GROUPS = 16

PAIR = 1
FLOWS_AHEAD = 2

QUANTISE_LAG = 1
ROOT_LAG = 1
TRANSPOSE_LAG = GROUP
COPY_LAG = GROUP + 1
MESSAGE_LAG = GROUP + 2
PACK_LAG = GROUP + 3
OUTPUT_LAG = GROUP + 4


def tile_encoder_flows_pb_t_kernel(tc, flows, x_gcn1, W2, b2, out):
    nc = tc.nc
    with ExitStack() as ctx:
        const = ctx.enter_context(tc.tile_pool(name="const", bufs=1))
        loaded = ctx.enter_context(tc.tile_pool(name="loaded", bufs=1))
        work = ctx.enter_context(tc.tile_pool(name="work", bufs=3))
        held = ctx.enter_context(tc.tile_pool(name="held", bufs=OUTPUT_LAG + 1))
        packed = ctx.enter_context(tc.tile_pool(name="packed", bufs=3))
        results = ctx.enter_context(tc.tile_pool(name="results", bufs=6))
        transposed_psum = ctx.enter_context(tc.psum_pool(name="transposed_psum", bufs=1))
        xw_psum = ctx.enter_context(tc.psum_pool(name="xw_psum", bufs=3))
        sum_psum = ctx.enter_context(tc.psum_pool(name="sum_psum", bufs=2))
        degree_psum = ctx.enter_context(tc.psum_pool(name="degree_psum", bufs=2))
        ctx.enter_context(tc.manual_schedule())

        raw = []
        x_rows = []
        x_view = x_gcn1.rearrange("g (p t) k -> p g t k", t=PACK)
        w2_sb = const.tile([FEAT, WIDTH], BF16)
        b2_row = const.tile([P, WIDTH], BF16)
        nc.vector.memset(b2_row[:], 0.0)
        for g in range(GRAPHS):
            raw_g = loaded.tile([P, PACK, NODES], BF16, name="raw%d" % g)
            nc.sync.dma_start(out=raw_g[:], in_=flows[g].rearrange("(p j) c -> p j c", j=PACK))
            raw.append(raw_g)
            if g == 0:
                nc.sync.dma_start(out=b2_row[0:1, :], in_=b2.rearrange("(o i) -> o i", o=1))
                nc.sync.dma_start(out=w2_sb[:], in_=W2)
            for q in range(GRAPHS // PAIR):
                if g == min(PAIR * (q + 1) - 1 + FLOWS_AHEAD, GRAPHS - 1):
                    x_q = loaded.tile([P, PAIR, PACK, FEAT], BF16, name="x_rows%d" % q)
                    nc.sync.dma_start(out=x_q[:], in_=x_view[:, q * PAIR : (q + 1) * PAIR])
                    x_rows.append(x_q)

        one_column = const.tile([P, 1], F32)
        nc.vector.memset(one_column[:], 1.0)
        root_of_one = const.tile([P, 1], F32)
        nc.scalar.activation(out=root_of_one[:], in_=one_column[:], func=ACT.Abs_reciprocal_sqrt)
        floor = const.tile([P, 1], F32)
        nc.vector.memset(floor[:], FLOOR)

        identity_bf16 = const.tile([P, P], BF16)
        make_identity(nc, identity_bf16[:])
        ones_bf16 = const.tile([P, P], BF16)
        nc.vector.memset(ones_bf16[:], 1.0)

        bias = const.tile([P, WIDTH], F32)

        def spread_bias():
            spread = xw_psum.tile([P, 2, WIDTH], F32, tag="xw", name="spread_bias")
            nc.tensor.matmul(out=spread[:, 0, :], lhsT=ones_bf16[:], rhs=b2_row[:], start=True, stop=True)
            nc.vector.tensor_copy(out=bias[:], in_=spread[:, 0, :])

        degrees = {}
        flows_grouped = {}
        msg_grouped = {}
        roots = {}
        dinv = {}
        flow_codes = {}
        flow_scales = {}
        x_transposed_psum = {}
        x_transposed = {}
        xw = {}
        msg_rows = {}
        msg_codes = {}
        msg_scales = {}
        sums = {}

        def add_up_degrees(g):
            if g % GROUP == 0:
                degree_tile = degree_psum.tile([P, GROUP * PACK], F32)
                degrees[g // GROUP] = degree_tile
            for t in range(PACK):
                column = (g % GROUP) * PACK + t
                for j in range(PACK):
                    nc.tensor.matmul(
                        out=degrees[g // GROUP][:, column : column + 1],
                        lhsT=raw[g][:, j, t :: PACK],
                        rhs=ones_bf16[:, 0:1],
                        start=(j == 0),
                        stop=(j == PACK - 1),
                    )

        def regrouping_views(g):
            to = flows_grouped[g][:].rearrange("p t m j -> p m j t")
            source = raw[g][:].rearrange("p j (m t) -> p m j t", t=PACK)
            if g < MESSAGE_LAG:
                vector_columns = EARLY_COLUMNS
            elif g < OUTPUT_LAG:
                vector_columns = MIDDLE_COLUMNS
            else:
                vector_columns = LATE_COLUMNS
            return to, source, vector_columns, vector_columns + (GPSIMD_COLUMNS if g >= OUTPUT_LAG else 0)

        def regroup_flows_on_scalar(g):
            grouped = work.tile([P, PACK, P, PACK], BF16, align_bytes=64, name="flows_grouped")
            flows_grouped[g] = grouped
            to, source, vector_columns, first = regrouping_views(g)
            nc.scalar.copy(out=to[:, first:], in_=source[:, first:])
            if first > vector_columns:
                nc.gpsimd.tensor_scalar(
                    out=to[:, vector_columns:first],
                    in0=source[:, vector_columns:first],
                    scalar1=1.0,
                    scalar2=0.0,
                    op0=ALU.mult,
                    op1=ALU.add,
                )

        def regroup_flows_on_vector(g):
            to, source, vector_columns, first = regrouping_views(g)
            nc.vector.tensor_copy(out=to[:, :vector_columns], in_=source[:, :vector_columns])

        def quantise_flows(g):
            codes = held.tile([P, NODES], U32, align_bytes=64, name="flow_codes")
            scales = held.tile([P, NODES], U8, align_bytes=64, name="flow_scales")
            nc.vector.quantize_mx(
                out=codes[:].bitcast(FP8X4), scales=scales[:], in_=flows_grouped[g][:].rearrange("p t m j -> p (t m j)")
            )
            flow_codes[g] = codes
            flow_scales[g] = scales

        def take_inverse_roots(q):
            root = work.tile([P, GROUP * PACK], F32, name="inverse_root")
            nc.scalar.activation(
                out=root[:], in_=degrees[q][:], func=ACT.Abs_reciprocal_sqrt, bias=floor[:]
            )
            roots[q] = root

        def zero_empty_nodes(q):
            dinv_q = const.tile([P, GROUP * PACK], F32, name="dinv%d" % q)
            nc.vector.scalar_tensor_tensor(
                out=dinv_q[:], in0=degrees[q][:], scalar=0.0, in1=roots[q][:], op0=ALU.is_gt, op1=ALU.mult
            )
            dinv[q] = dinv_q

        def dinv_column(g, t):
            column = (g % GROUP) * PACK + t
            return dinv[g // GROUP][:, column : column + 1]

        def transpose_x(g):
            flipped = transposed_psum.tile([FEAT, PACK, P], BF16)
            for t in range(PACK):
                nc.tensor.transpose(
                    out=flipped[:, t, :], in_=x_rows[g // PAIR][:, g % PAIR, t, :], identity=identity_bf16[:]
                )
            x_transposed_psum[g] = flipped

        def copy_transposed_x(g):
            copied = work.tile([FEAT, PACK, P], BF16, name="x_transposed")
            nc.scalar.copy(out=copied[:], in_=x_transposed_psum[g][:])
            x_transposed[g] = copied

        def multiply_by_w2(g):
            xw[g] = []
            for half in range(2):
                bank = xw_psum.tile([P, 2, WIDTH], F32, tag="xw", name="xw_bank")
                for u in range(2):
                    nc.tensor.matmul(
                        out=bank[:, u, :], lhsT=x_transposed[g][:, 2 * half + u, :], rhs=w2_sb[:], start=True, stop=True
                    )
                xw[g].append(bank)

        def scale_messages(g):
            rows = work.tile([P, PACK, WIDTH], BF16, name="msg_rows")
            for t in range(PACK):
                nc.scalar.activation(
                    out=rows[:, t, :], in_=xw[g][t // 2][:, t % 2, :], func=ACT.Copy, scale=dinv_column(g, t)
                )
            msg_rows[g] = rows

        def regroup_messages(g):
            grouped = work.tile([P, WIDTH, PACK], BF16, align_bytes=64, name="msg_grouped")
            to = grouped[:].rearrange("p (c i) t -> p c t i", i=4)
            source = msg_rows[g][:].rearrange("p t (c i) -> p c t i", i=4)
            if g == LAST:
                vector_groups = 0
            elif g + PACK_LAG >= GRAPHS:
                vector_groups = WIDTH // 4 - SCALAR_GROUPS
            else:
                vector_groups = WIDTH // 4
            if vector_groups > 0:
                nc.vector.tensor_copy(out=to[:, :vector_groups], in_=source[:, :vector_groups])
            if vector_groups < WIDTH // 4:
                nc.scalar.copy(out=to[:, vector_groups:], in_=source[:, vector_groups:])
            msg_grouped[g] = grouped

        def quantise_messages(g):
            codes = packed.tile([P, WIDTH], U32, align_bytes=64, name="msg_codes")
            scales = packed.tile([P, WIDTH], U8, align_bytes=64, name="msg_scales")
            nc.vector.quantize_mx(
                out=codes[:].bitcast(FP8X4), scales=scales[:], in_=msg_grouped[g][:].rearrange("p i t -> p (i t)")
            )
            msg_codes[g] = codes
            msg_scales[g] = scales

        def contract(g):
            sums[g] = []
            for half in range(2):
                bank = sum_psum.tile([P, 2, WIDTH], F32, name="sum_bank")
                for u in range(2):
                    lane = slice((2 * half + u) * P, (2 * half + u + 1) * P)
                    nc.tensor.matmul_mx(
                        out=bank[:, u, :],
                        lhsT=flow_codes[g][:, lane].bitcast(FP8X4),
                        lhsT_scale=flow_scales[g][:, lane],
                        rhs=msg_codes[g][:].bitcast(FP8X4),
                        rhs_scale=msg_scales[g][:],
                        start=True,
                        stop=True,
                    )
                sums[g].append(bank)

        def finish(g):
            result = results.tile([P, PACK, WIDTH], F32)
            for t in range(PACK):
                nc.vector.scalar_tensor_tensor(
                    out=result[:, t, :],
                    in0=sums[g][t // 2][:, t % 2, :],
                    scalar=dinv_column(g, t),
                    in1=bias[:],
                    op0=ALU.mult,
                    op1=ALU.add,
                )
                if t % 2 == 1:
                    lanes = slice(t - 1, t + 1)
                    nc.sync.dma_start(out=out[g].rearrange("(p t) i -> p t i", t=PACK)[:, lanes], in_=result[:, lanes])

        def graph_at(k, lag):
            return k - lag if 0 <= k - lag < GRAPHS else None

        def group_at(k, lag):
            g = graph_at(k, lag)
            return g // GROUP if g is not None and g % GROUP == GROUP - 1 else None

        for k in range(GRAPHS + OUTPUT_LAG):
            g_regroup = graph_at(k, 0)
            g_quantise = graph_at(k, QUANTISE_LAG)
            q_root = group_at(k, ROOT_LAG)
            g_transpose = graph_at(k, TRANSPOSE_LAG)
            g_copy = graph_at(k, COPY_LAG)
            g_message = graph_at(k, MESSAGE_LAG)
            g_pack = graph_at(k, PACK_LAG)
            g_output = graph_at(k, OUTPUT_LAG)

            if k == 1:
                spread_bias()
            if g_regroup is not None:
                regroup_flows_on_scalar(g_regroup)
            if g_copy is not None:
                copy_transposed_x(g_copy)
            if q_root is not None:
                take_inverse_roots(q_root)
            if g_pack == LAST:
                regroup_messages(LAST)
            if g_output is not None and g_output != LAST:
                quantise_messages(g_output)
            if g_pack == LAST:
                quantise_messages(LAST)
            if g_quantise is not None:
                quantise_flows(g_quantise)
            if g_message is not None:
                multiply_by_w2(g_message)
            if g_output is not None:
                contract(g_output)
            if g_regroup is not None:
                add_up_degrees(g_regroup)
            if g_transpose is not None:
                transpose_x(g_transpose)
            if g_message is not None:
                scale_messages(g_message)
            if g_regroup is not None:
                regroup_flows_on_vector(g_regroup)
            if g_pack is not None and g_pack != LAST:
                regroup_messages(g_pack)
            if g_output is not None:
                finish(g_output)
            if q_root is not None:
                zero_empty_nodes(q_root)
